import numpy as np
import ml_dtypes


def mxq(x, axis, fmt="e4m3"):
    dtype, down = {"e4m3": (ml_dtypes.float8_e4m3fn, 7), "e5m2": (ml_dtypes.float8_e5m2, 14)}[fmt]
    v = np.moveaxis(np.asarray(x, np.float32).astype(ml_dtypes.bfloat16).astype(np.float64), axis, -1)
    blocks = v.reshape(v.shape[:-1] + (-1, 32))
    amax = np.abs(blocks).max(-1, keepdims=True)
    byte = np.maximum(np.where(amax > 0, np.frexp(amax)[1] - 1 + 127, 0) - down, 1)
    scale = np.exp2(byte - 127.0)
    codes = (blocks / scale).astype(np.float32).astype(dtype).astype(np.float64)
    return np.moveaxis((codes * scale).reshape(v.shape), -1, axis)


WIDE = False


def mx_kscale(k):
    if not WIDE:
        return np.ones(k)
    levels = np.array([10, -10, 5, -5, 0])
    a = np.random.permutation(np.resize(levels, k // 512 * 4)).reshape(k // 512, 4)
    idx = np.arange(k)
    return np.exp2(a[idx // 512, idx % 128 // 32])


BF16 = ml_dtypes.bfloat16


def bf(x):
    return np.asarray(x, np.float32).astype(BF16)


def f64(x):
    return np.asarray(x).astype(np.float64)


E2M1 = np.array([0.0, 0.5, 1.0, 1.5, 2.0, 3.0, 4.0, 6.0, -0.0, -0.5, -1.0, -1.5, -2.0, -3.0, -4.0, -6.0])


def pack_weight(w, fmt):
    k, n = w.shape
    w = f64(bf(w)).reshape(k // 32, 32, n)
    amax = np.abs(w).max(1)
    if fmt == "e4m3":
        byte = np.frexp(amax)[1] - 1 + 127 - 7
    else:
        mant, ex = np.frexp(amax / 6.0)
        byte = np.where(mant > 0.5, ex, ex - 1) + 127
    byte = np.clip(np.where(amax > 0, byte, 1), 1, 254)
    scaled = (w * np.exp2(127.0 - byte)[:, None, :]).reshape(k, n).astype(np.float32)
    by_word = np.ascontiguousarray(scaled.reshape(k // 512, 128, 4, n).transpose(0, 1, 3, 2))
    if fmt == "e4m3":
        words = by_word.astype(ml_dtypes.float8_e4m3fn).view(np.uint8)
    else:
        c = by_word.astype(ml_dtypes.float4_e2m1fn).view(np.uint8) & 0xF
        words = c[..., 0::2] | (c[..., 1::2] << 4)
    return np.ascontiguousarray(words), np.ascontiguousarray(byte.astype(np.uint8).reshape(k // 512, 16, n))


def unpack_weight(words, scales, fmt):
    g, p, n, _ = words.shape
    if fmt == "e4m3":
        vals = np.ascontiguousarray(words).view(ml_dtypes.float8_e4m3fn).astype(np.float64)
    else:
        nib = np.empty((g, p, n, 4), np.uint8)
        nib[..., 0::2] = words & 0xF
        nib[..., 1::2] = words >> 4
        vals = E2M1[nib]
    vals = vals * np.repeat(np.exp2(scales.astype(np.float64) - 127.0), 8, axis=1)[..., None]
    return vals.transpose(0, 1, 3, 2).reshape(g * 512, n)


B, HH, WW, C, NH, DIM = 2, 8, 16, 16384, 8, 32
N = HH * WW
HD = NH * DIM
F = 4 * HD
BN_EPS = 1e-5
WS = 0.02
GQK = np.sqrt(2.8) / DIM ** 0.25
GV = 4.0


def heads(t):
    return t.reshape(B, N, NH, DIM).transpose(0, 2, 1, 3)


def setup_inputs():
    s = mx_kscale(C)
    x = np.random.standard_normal((B, HH, WW, C)) + 0.5 * np.random.standard_normal(C)
    gain = np.concatenate([np.full(2 * HD, GQK), np.full(2 * HD, GV)])
    inputs = bf(x * s)
    words, scales = pack_weight(np.random.standard_normal((C, F)) * WS / np.sqrt(C) / s[:, None], "e4m3")
    return {"inputs": inputs,
            "w_qkv_words": words,
            "w_qkv_scales": scales,
            "bn_scale": bf(np.random.standard_normal(F) * gain)}


def reference(inputs, w_qkv_words, w_qkv_scales, bn_scale):
    x = mxq(f64(inputs).reshape(B * N, C), 1, "e4m3") @ unpack_weight(w_qkv_words, w_qkv_scales, "e4m3")
    mean = x.mean(axis=0)
    var = x.var(axis=0)
    x = (x - mean) / np.sqrt(var + BN_EPS) * f64(bn_scale)
    q, k, v1, v2 = (heads(t) for t in np.split(x.reshape(B, N, F), 4, axis=-1))
    v = np.concatenate((v1, v2), axis=-1)
    return np.ascontiguousarray(q), np.ascontiguousarray(k), v

@@ -1,0 +1,235 @@
+from contextlib import ExitStack
+
+import concourse.mybir as mybir
+from concourse.masks import make_identity
+
+F32 = mybir.dt.float32
+BF16 = mybir.dt.bfloat16
+I32 = mybir.dt.int32
+U32 = mybir.dt.uint32
+U8 = mybir.dt.uint8
+FP8X4 = mybir.dt.float8_e4m3fn_x4
+ALU = mybir.AluOpType
+ACT = mybir.ActivationFunctionType
+
+P = 128
+MAPS = 2
+PIXELS = MAPS * P
+CHANNELS = 16384
+COLUMNS = 1024
+HEAD_DIM = 32
+BN_EPS = 1e-5
+
+GROUP = 4 * P
+GROUPS = CHANNELS // GROUP
+GROUP_WORDS = GROUP // 2
+CHUNK_GROUPS = 4
+CHUNKS = GROUPS // CHUNK_GROUPS
+COLUMN_TILES = COLUMNS // P
+QUARTERS = 4
+QUARTER = COLUMNS // QUARTERS
+TILES_PER_QUARTER = QUARTER // P
+PLANES_PER_TILE = 4
+
+W_LOAD_GROUPS = 2
+LAST_GROUPS = 4
+STREAM_GROUPS = GROUPS - LAST_GROUPS
+W_LOADS = STREAM_GROUPS // W_LOAD_GROUPS
+
+X_BUFS = 6
+W_BUFS = 8
+
+FLOPS = 2 * PIXELS * CHANNELS * COLUMNS
+
+
+def tile_levitattention_pa_k_kernel(tc, inputs, w_qkv_words, w_qkv_scales, bn_scale, out_0, out_1, out_2):
+    nc = tc.nc
+
+    x_rows = inputs.rearrange("b h w c -> (h w) b c")
+    w_words = w_qkv_words.rearrange("g p n t -> g p (n t)").bitcast(I32)
+    w_scale_rows = w_qkv_scales.bitcast(I32)
+    quarter_out = [
+        out_0.rearrange("b h n d -> n (b h) d"),
+        out_1.rearrange("b h n d -> n (b h) d"),
+        out_2[:, :, :, 0:HEAD_DIM].rearrange("b h n d -> n (b h) d"),
+        out_2[:, :, :, HEAD_DIM : 2 * HEAD_DIM].rearrange("b h n d -> n (b h) d"),
+    ]
+
+    with ExitStack() as ctx:
+        ctx.enter_context(tc.manual_schedule())
+        keep = ctx.enter_context(tc.tile_pool(name="keep", bufs=1))
+        x_pool = ctx.enter_context(tc.tile_pool(name="x_pool", bufs=X_BUFS))
+        grouped_pool = ctx.enter_context(tc.tile_pool(name="grouped_pool", bufs=3))
+        w_pool = ctx.enter_context(tc.tile_pool(name="w_pool", bufs=W_BUFS))
+        last_pool = ctx.enter_context(tc.tile_pool(name="last_pool", bufs=QUARTERS))
+        psum = ctx.enter_context(tc.psum_pool(name="psum", bufs=8))
+
+        x_codes = keep.tile([P, GROUPS, PIXELS], U32, align_bytes=64)
+        x_scales = keep.tile([P, GROUPS, PIXELS], U8, align_bytes=64)
+        w_planes = keep.tile([P, GROUPS // PLANES_PER_TILE, COLUMNS], U8, align_bytes=64)
+
+        nc.vector.memset(w_planes[:].bitcast(I32), 0)
+
+        def load_chunk(c):
+            x_raw = x_pool.tile([P, MAPS, CHUNK_GROUPS * GROUP], BF16, name="x_raw")
+            first = c * CHUNK_GROUPS * GROUP
+            nc.sync.dma_start(out=x_raw[:], in_=x_rows[:, :, first : first + CHUNK_GROUPS * GROUP])
+            return x_raw
+
+        def load_scale_slot(slot):
+            first = slot * PLANES_PER_TILE
+            for quadrant in range(4):
+                nc.sync.dma_start(
+                    out=w_planes[32 * quadrant : 32 * quadrant + 16, slot, :].bitcast(I32),
+                    in_=w_scale_rows[first : first + PLANES_PER_TILE, 4 * quadrant : 4 * quadrant + 4, :],
+                )
+
+        def load_weights(i):
+            w_tile = w_pool.tile([P, W_LOAD_GROUPS, COLUMNS], U32, name="w_tile", align_bytes=64)
+            first = i * W_LOAD_GROUPS
+            nc.sync.dma_start(
+                out=w_tile[:].bitcast(I32),
+                in_=w_words[first : first + W_LOAD_GROUPS].rearrange("g p n -> p g n"),
+            )
+            return w_tile
+
+        def load_last_weights(quarter):
+            w_last = last_pool.tile([P, LAST_GROUPS, QUARTER], U32, name="w_last", align_bytes=64)
+            nc.sync.dma_start(
+                out=w_last[:].bitcast(I32),
+                in_=w_words[STREAM_GROUPS:GROUPS, :, quarter * QUARTER : (quarter + 1) * QUARTER].rearrange(
+                    "g p n -> p g n"
+                ),
+            )
+            return w_last
+
+        chunks = []
+        for c in range(X_BUFS):
+            chunks.append(load_chunk(c))
+            load_scale_slot(c)
+
+        identity = keep.tile([P, P], F32)
+        make_identity(nc, identity[:])
+        gain_rows = keep.tile([P, P], BF16)
+        nc.vector.memset(gain_rows[:], 0.0)
+        nc.scalar.dma_start(out=gain_rows[0:COLUMN_TILES, :], in_=bn_scale.rearrange("(j p) -> j p", p=P))
+        eps = keep.tile([P, 1], F32)
+        nc.vector.memset(eps[:], BN_EPS)
+        table_warmer = keep.tile([P, 1], F32)
+        nc.scalar.sqrt(out=table_warmer[:], in_=eps[:])
+        gain_rows_f32 = keep.tile([P, P], F32)
+        nc.vector.tensor_copy(out=gain_rows_f32[:], in_=gain_rows[:])
+        gain_turned = psum.tile([P, P], F32, tag="bank", name="gain_turned")
+        nc.tensor.transpose(gain_turned[:], gain_rows_f32[:], identity[:])
+        gain = keep.tile([P, COLUMN_TILES], F32)
+        nc.vector.tensor_copy(out=gain[:], in_=gain_turned[:, 0:COLUMN_TILES])
+
+        def quantise_chunk(c, grouped):
+            groups = slice(c * CHUNK_GROUPS, (c + 1) * CHUNK_GROUPS)
+            nc.vector.quantize_mx(
+                out=x_codes[:, groups, :].rearrange("p g r -> p (g r)").bitcast(FP8X4),
+                scales=x_scales[:, groups, :].rearrange("p g r -> p (g r)"),
+                in_=grouped[:],
+            )
+
+        grouped_before = None
+        for c in range(CHUNKS):
+            if grouped_before is not None:
+                quantise_chunk(c - 1, grouped_before)
+            x_raw = chunks[c]
+            grouped = grouped_pool.tile([P, CHUNK_GROUPS * PIXELS * 4], BF16, name="grouped", align_bytes=64)
+            for k in range(CHUNK_GROUPS):
+                turned = psum.tile([P, 2, PIXELS], F32, tag="bank", name="turned")
+                for b in range(MAPS):
+                    words = x_raw[:, b, :].bitcast(F32)
+                    for u in range(2):
+                        nc.tensor.transpose(
+                            turned[:, u, b * P : (b + 1) * P],
+                            words[:, k * GROUP_WORDS + u : (k + 1) * GROUP_WORDS : 2],
+                            identity[:],
+                        )
+                pairs = grouped[:].bitcast(F32)[:, k * 2 * PIXELS : (k + 1) * 2 * PIXELS]
+                if k < CHUNK_GROUPS - 1:
+                    nc.scalar.copy(
+                        out=pairs.rearrange("p (r u) -> p r u", u=2), in_=turned[:].rearrange("p u r -> p r u")
+                    )
+                else:
+                    nc.vector.tensor_copy(
+                        out=pairs.rearrange("p (r u) -> p r u", u=2), in_=turned[:].rearrange("p u r -> p r u")
+                    )
+            grouped_before = grouped
+            if c + X_BUFS < CHUNKS:
+                chunks.append(load_chunk(c + X_BUFS))
+                load_scale_slot(c + X_BUFS)
+        quantise_chunk(CHUNKS - 1, grouped_before)
+
+        sums = [psum.tile([P, PIXELS], F32, tag="bank", name="sums%d" % j) for j in range(COLUMN_TILES)]
+
+        def mx_pass(g, j, w_columns):
+            plane = PLANES_PER_TILE * (g % PLANES_PER_TILE)
+            nc.tensor.matmul_mx(
+                out=sums[j][:],
+                lhsT=w_columns.bitcast(FP8X4),
+                lhsT_scale=w_planes[plane:P, g // PLANES_PER_TILE, j * P : (j + 1) * P],
+                rhs=x_codes[:, g, :].bitcast(FP8X4),
+                rhs_scale=x_scales[:, g, :],
+                start=(g == 0),
+                stop=(g == GROUPS - 1),
+            )
+
+        w_tiles = [load_weights(i) for i in range(W_BUFS)]
+        for i in range(W_LOADS):
+            for k in range(W_LOAD_GROUPS):
+                for j in range(COLUMN_TILES):
+                    mx_pass(i * W_LOAD_GROUPS + k, j, w_tiles[i][:, k, j * P : (j + 1) * P])
+            if i + W_BUFS < W_LOADS:
+                w_tiles.append(load_weights(i + W_BUFS))
+        w_lasts = [load_last_weights(quarter) for quarter in range(QUARTERS)]
+
+        def finish_sums(quarter):
+            w_last = w_lasts[quarter]
+            for i in range(TILES_PER_QUARTER):
+                for k in range(LAST_GROUPS):
+                    mx_pass(STREAM_GROUPS + k, quarter * TILES_PER_QUARTER + i, w_last[:, k, i * P : (i + 1) * P])
+
+        def normalise(quarter):
+            first = quarter * TILES_PER_QUARTER
+            stats = last_pool.tile([P, TILES_PER_QUARTER, 6], F32, name="stats")
+            mean_var = last_pool.tile([P, TILES_PER_QUARTER, 2], F32, name="mean_var")
+            for i in range(TILES_PER_QUARTER):
+                nc.vector.bn_stats(out=stats[:, i, :], in_=sums[first + i][:])
+                nc.vector.bn_aggr(out=mean_var[:, i, :], in_=stats[:, i, :])
+            std = last_pool.tile([P, TILES_PER_QUARTER], F32, name="std")
+            nc.scalar.activation(out=std[:], in_=mean_var[:, :, 1], func=ACT.Sqrt, bias=eps[:, 0:1], scale=1.0)
+            factor = last_pool.tile([P, TILES_PER_QUARTER], F32, name="factor")
+            nc.vector.reciprocal(out=factor[:], in_=std[:])
+            nc.vector.tensor_mul(out=factor[:], in0=factor[:], in1=gain[:, first : first + TILES_PER_QUARTER])
+            normed = last_pool.tile([P, TILES_PER_QUARTER, PIXELS], F32, name="normed")
+            for i in range(TILES_PER_QUARTER):
+                nc.vector.tensor_scalar(
+                    out=normed[:, i, :],
+                    in0=sums[first + i][:],
+                    scalar1=mean_var[:, i, 0:1],
+                    scalar2=factor[:, i : i + 1],
+                    op0=ALU.subtract,
+                    op1=ALU.mult,
+                )
+            return normed
+
+        def turn_back_and_store(quarter, normed):
+            back = psum.tile([P, MAPS, QUARTER], F32, tag="bank", name="back")
+            for i in range(TILES_PER_QUARTER):
+                for b in range(MAPS):
+                    nc.tensor.transpose(back[:, b, i * P : (i + 1) * P], normed[:, i, b * P : (b + 1) * P], identity[:])
+            result = last_pool.tile([P, MAPS, QUARTER], F32, name="result")
+            nc.scalar.copy(out=result[:], in_=back[:])
+            nc.sync.dma_start(
+                out=quarter_out[quarter], in_=result[:].rearrange("n b (h d) -> n (b h) d", d=HEAD_DIM)
+            )
+
+        finish_sums(0)
+        for quarter in range(QUARTERS):
+            normed = normalise(quarter)
+            if quarter + 1 < QUARTERS:
+                finish_sums(quarter + 1)
+            turn_back_and_store(quarter, normed)

@@ -47,7 +47,7 @@ def tile_levitattention_pa_k_kernel(tc, inputs, w_qkv_words, w_qkv_scales, bn_sc
 
     x_rows = inputs.rearrange("b h w c -> (h w) b c")
     w_words = w_qkv_words.rearrange("g p n t -> g p (n t)").bitcast(I32)
-    w_scale_rows = w_qkv_scales.bitcast(I32)
+    w_scale_rows = w_qkv_scales.bitcast(F32)
     quarter_out = [
         out_0.rearrange("b h n d -> n (b h) d"),
         out_1.rearrange("b h n d -> n (b h) d"),
@@ -79,8 +79,8 @@ def tile_levitattention_pa_k_kernel(tc, inputs, w_qkv_words, w_qkv_scales, bn_sc
         def load_scale_slot(slot):
             first = slot * PLANES_PER_TILE
             for quadrant in range(4):
-                nc.sync.dma_start(
-                    out=w_planes[32 * quadrant : 32 * quadrant + 16, slot, :].bitcast(I32),
+                nc.gpsimd.dma_start(
+                    out=w_planes[32 * quadrant : 32 * quadrant + 16, slot, :].bitcast(F32),
                     in_=w_scale_rows[first : first + PLANES_PER_TILE, 4 * quadrant : 4 * quadrant + 4, :],
                 )
 
@@ -106,10 +106,11 @@ def tile_levitattention_pa_k_kernel(tc, inputs, w_qkv_words, w_qkv_scales, bn_sc
         chunks = []
         for c in range(X_BUFS):
             chunks.append(load_chunk(c))
-            load_scale_slot(c)
 
         identity = keep.tile([P, P], F32)
         make_identity(nc, identity[:])
+        for slot in range(GROUPS // PLANES_PER_TILE):
+            load_scale_slot(slot)
         gain_rows = keep.tile([P, P], BF16)
         nc.vector.memset(gain_rows[:], 0.0)
         nc.scalar.dma_start(out=gain_rows[0:COLUMN_TILES, :], in_=bn_scale.rearrange("(j p) -> j p", p=P))
@@ -160,7 +161,6 @@ def tile_levitattention_pa_k_kernel(tc, inputs, w_qkv_words, w_qkv_scales, bn_sc
             grouped_before = grouped
             if c + X_BUFS < CHUNKS:
                 chunks.append(load_chunk(c + X_BUFS))
-                load_scale_slot(c + X_BUFS)
         quantise_chunk(CHUNKS - 1, grouped_before)
 
         sums = [psum.tile([P, PIXELS], F32, tag="bank", name="sums%d" % j) for j in range(COLUMN_TILES)]

@@ -17,6 +17,7 @@ MAPS = 2
 PIXELS = MAPS * P
 CHANNELS = 16384
 COLUMNS = 1024
+HEADS = 8
 HEAD_DIM = 32
 BN_EPS = 1e-5
 
@@ -48,12 +49,6 @@ def tile_levitattention_pa_k_kernel(tc, inputs, w_qkv_words, w_qkv_scales, bn_sc
     x_rows = inputs.rearrange("b h w c -> (h w) b c")
     w_words = w_qkv_words.rearrange("g p n t -> g p (n t)").bitcast(I32)
     w_scale_rows = w_qkv_scales.bitcast(F32)
-    quarter_out = [
-        out_0.rearrange("b h n d -> n (b h) d"),
-        out_1.rearrange("b h n d -> n (b h) d"),
-        out_2[:, :, :, 0:HEAD_DIM].rearrange("b h n d -> n (b h) d"),
-        out_2[:, :, :, HEAD_DIM : 2 * HEAD_DIM].rearrange("b h n d -> n (b h) d"),
-    ]
 
     with ExitStack() as ctx:
         ctx.enter_context(tc.manual_schedule())
@@ -186,34 +181,46 @@ def tile_levitattention_pa_k_kernel(tc, inputs, w_qkv_words, w_qkv_scales, bn_sc
                 w_tiles.append(load_weights(i + W_BUFS))
         w_lasts = [load_last_weights(quarter) for quarter in range(QUARTERS)]
 
-        def finish_sums(quarter):
-            w_last = w_lasts[quarter]
-            for i in range(TILES_PER_QUARTER):
-                for k in range(LAST_GROUPS):
-                    mx_pass(STREAM_GROUPS + k, quarter * TILES_PER_QUARTER + i, w_last[:, k, i * P : (i + 1) * P])
+        result_q = keep.tile([P, MAPS * HEADS, HEAD_DIM], F32)
+        result_k = keep.tile([P, MAPS * HEADS, HEAD_DIM], F32)
+        result_v = keep.tile([P, MAPS * HEADS, 2 * HEAD_DIM], F32)
+        quarter_result = [result_q[:], result_k[:], result_v[:, :, 0:HEAD_DIM], result_v[:, :, HEAD_DIM : 2 * HEAD_DIM]]
+        complete_after = {0: (out_0, result_q), 1: (out_1, result_k), 3: (out_2, result_v)}
 
-        def normalise(quarter):
+        def finish_and_measure(quarter):
             first = quarter * TILES_PER_QUARTER
             stats = last_pool.tile([P, TILES_PER_QUARTER, 6], F32, name="stats")
             mean_var = last_pool.tile([P, TILES_PER_QUARTER, 2], F32, name="mean_var")
             for i in range(TILES_PER_QUARTER):
+                for k in range(LAST_GROUPS):
+                    mx_pass(STREAM_GROUPS + k, first + i, w_lasts[quarter][:, k, i * P : (i + 1) * P])
                 nc.vector.bn_stats(out=stats[:, i, :], in_=sums[first + i][:])
                 nc.vector.bn_aggr(out=mean_var[:, i, :], in_=stats[:, i, :])
             std = last_pool.tile([P, TILES_PER_QUARTER], F32, name="std")
             nc.scalar.activation(out=std[:], in_=mean_var[:, :, 1], func=ACT.Sqrt, bias=eps[:, 0:1], scale=1.0)
+            return mean_var, std
+
+        def normalise(quarter, mean_var, std):
+            first = quarter * TILES_PER_QUARTER
             factor = last_pool.tile([P, TILES_PER_QUARTER], F32, name="factor")
+            shift = last_pool.tile([P, TILES_PER_QUARTER], F32, name="shift")
             nc.vector.reciprocal(out=factor[:], in_=std[:])
             nc.vector.tensor_mul(out=factor[:], in0=factor[:], in1=gain[:, first : first + TILES_PER_QUARTER])
+            nc.vector.scalar_tensor_tensor(
+                out=shift[:], in0=mean_var[:, :, 0], scalar=-1.0, in1=factor[:], op0=ALU.mult, op1=ALU.mult
+            )
             normed = last_pool.tile([P, TILES_PER_QUARTER, PIXELS], F32, name="normed")
-            for i in range(TILES_PER_QUARTER):
-                nc.vector.tensor_scalar(
-                    out=normed[:, i, :],
-                    in0=sums[first + i][:],
-                    scalar1=mean_var[:, i, 0:1],
-                    scalar2=factor[:, i : i + 1],
-                    op0=ALU.subtract,
-                    op1=ALU.mult,
-                )
+            nc.vector.tensor_scalar(
+                out=normed[:, 0, :],
+                in0=sums[first][:],
+                scalar1=factor[:, 0:1],
+                scalar2=shift[:, 0:1],
+                op0=ALU.mult,
+                op1=ALU.add,
+            )
+            nc.scalar.activation(
+                out=normed[:, 1, :], in_=sums[first + 1][:], func=ACT.Identity, bias=shift[:, 1:2], scale=factor[:, 1:2]
+            )
             return normed
 
         def turn_back_and_store(quarter, normed):
@@ -221,15 +228,18 @@ def tile_levitattention_pa_k_kernel(tc, inputs, w_qkv_words, w_qkv_scales, bn_sc
             for i in range(TILES_PER_QUARTER):
                 for b in range(MAPS):
                     nc.tensor.transpose(back[:, b, i * P : (i + 1) * P], normed[:, i, b * P : (b + 1) * P], identity[:])
-            result = last_pool.tile([P, MAPS, QUARTER], F32, name="result")
-            nc.scalar.copy(out=result[:], in_=back[:])
-            nc.sync.dma_start(
-                out=quarter_out[quarter], in_=result[:].rearrange("n b (h d) -> n (b h) d", d=HEAD_DIM)
-            )
+            nc.scalar.copy(out=quarter_result[quarter], in_=back[:].rearrange("n b (h d) -> n (b h) d", d=HEAD_DIM))
+            if quarter in complete_after:
+                out, result = complete_after[quarter]
+                nc.sync.dma_start(out=out.rearrange("b h n d -> n (b h) d"), in_=result[:])
 
-        finish_sums(0)
-        for quarter in range(QUARTERS):
-            normed = normalise(quarter)
-            if quarter + 1 < QUARTERS:
-                finish_sums(quarter + 1)
-            turn_back_and_store(quarter, normed)
+        measures = {}
+        normed_tiles = {}
+        for step in range(QUARTERS + 2):
+            if step < QUARTERS:
+                measures[step] = finish_and_measure(step)
+            if 0 <= step - 1 < QUARTERS:
+                mean_var, std = measures[step - 1]
+                normed_tiles[step - 1] = normalise(step - 1, mean_var, std)
+            if 0 <= step - 2 < QUARTERS:
+                turn_back_and_store(step - 2, normed_tiles[step - 2])

@@ -63,12 +63,17 @@ def tile_levitattention_pa_k_kernel(tc, inputs, w_qkv_words, w_qkv_scales, bn_sc
         x_scales = keep.tile([P, GROUPS, PIXELS], U8, align_bytes=64)
         w_planes = keep.tile([P, GROUPS // PLANES_PER_TILE, COLUMNS], U8, align_bytes=64)
 
+        gain_rows = keep.tile([P, P], BF16)
+        nc.vector.memset(gain_rows[:], 0.0)
+        eps = keep.tile([P, 1], F32)
+        nc.vector.memset(eps[:], BN_EPS)
         nc.vector.memset(w_planes[:].bitcast(I32), 0)
 
         def load_chunk(c):
-            x_raw = x_pool.tile([P, MAPS, CHUNK_GROUPS * GROUP], BF16, name="x_raw")
             first = c * CHUNK_GROUPS * GROUP
-            nc.sync.dma_start(out=x_raw[:], in_=x_rows[:, :, first : first + CHUNK_GROUPS * GROUP])
+            x_raw = [x_pool.tile([P, CHUNK_GROUPS * GROUP], BF16, name="x_raw%d" % b) for b in range(MAPS)]
+            for b in range(MAPS):
+                nc.sync.dma_start(out=x_raw[b][:], in_=x_rows[:, b, first : first + CHUNK_GROUPS * GROUP])
             return x_raw
 
         def load_scale_slot(slot):
@@ -104,21 +109,13 @@ def tile_levitattention_pa_k_kernel(tc, inputs, w_qkv_words, w_qkv_scales, bn_sc
 
         identity = keep.tile([P, P], F32)
         make_identity(nc, identity[:])
+        identity_bf16 = keep.tile([P, P], BF16)
+        make_identity(nc, identity_bf16[:])
         for slot in range(GROUPS // PLANES_PER_TILE):
             load_scale_slot(slot)
-        gain_rows = keep.tile([P, P], BF16)
-        nc.vector.memset(gain_rows[:], 0.0)
         nc.scalar.dma_start(out=gain_rows[0:COLUMN_TILES, :], in_=bn_scale.rearrange("(j p) -> j p", p=P))
-        eps = keep.tile([P, 1], F32)
-        nc.vector.memset(eps[:], BN_EPS)
         table_warmer = keep.tile([P, 1], F32)
         nc.scalar.sqrt(out=table_warmer[:], in_=eps[:])
-        gain_rows_f32 = keep.tile([P, P], F32)
-        nc.vector.tensor_copy(out=gain_rows_f32[:], in_=gain_rows[:])
-        gain_turned = psum.tile([P, P], F32, tag="bank", name="gain_turned")
-        nc.tensor.transpose(gain_turned[:], gain_rows_f32[:], identity[:])
-        gain = keep.tile([P, COLUMN_TILES], F32)
-        nc.vector.tensor_copy(out=gain[:], in_=gain_turned[:, 0:COLUMN_TILES])
 
         def quantise_chunk(c, grouped):
             groups = slice(c * CHUNK_GROUPS, (c + 1) * CHUNK_GROUPS)
@@ -132,30 +129,35 @@ def tile_levitattention_pa_k_kernel(tc, inputs, w_qkv_words, w_qkv_scales, bn_sc
         for c in range(CHUNKS):
             if grouped_before is not None:
                 quantise_chunk(c - 1, grouped_before)
-            x_raw = chunks[c]
-            grouped = grouped_pool.tile([P, CHUNK_GROUPS * PIXELS * 4], BF16, name="grouped", align_bytes=64)
-            for k in range(CHUNK_GROUPS):
-                turned = psum.tile([P, 2, PIXELS], F32, tag="bank", name="turned")
-                for b in range(MAPS):
-                    words = x_raw[:, b, :].bitcast(F32)
+            turned = [psum.tile([P, 2, PIXELS], F32, tag="bank", name="turned%d" % k) for k in range(CHUNK_GROUPS)]
+            for b in range(MAPS):
+                words = chunks[c][b][:].bitcast(F32)
+                for k in range(CHUNK_GROUPS):
                     for u in range(2):
                         nc.tensor.transpose(
-                            turned[:, u, b * P : (b + 1) * P],
+                            turned[k][:, u, b * P : (b + 1) * P],
                             words[:, k * GROUP_WORDS + u : (k + 1) * GROUP_WORDS : 2],
                             identity[:],
                         )
+            grouped = grouped_pool.tile([P, CHUNK_GROUPS * PIXELS * 4], BF16, name="grouped", align_bytes=64)
+            for k in range(CHUNK_GROUPS):
                 pairs = grouped[:].bitcast(F32)[:, k * 2 * PIXELS : (k + 1) * 2 * PIXELS]
                 if k < CHUNK_GROUPS - 1:
                     nc.scalar.copy(
-                        out=pairs.rearrange("p (r u) -> p r u", u=2), in_=turned[:].rearrange("p u r -> p r u")
+                        out=pairs.rearrange("p (r u) -> p r u", u=2), in_=turned[k][:].rearrange("p u r -> p r u")
                     )
                 else:
                     nc.vector.tensor_copy(
-                        out=pairs.rearrange("p (r u) -> p r u", u=2), in_=turned[:].rearrange("p u r -> p r u")
+                        out=pairs.rearrange("p (r u) -> p r u", u=2), in_=turned[k][:].rearrange("p u r -> p r u")
                     )
             grouped_before = grouped
             if c + X_BUFS < CHUNKS:
                 chunks.append(load_chunk(c + X_BUFS))
+
+        gain_turned = psum.tile([P, P], BF16, tag="bank", name="gain_turned")
+        nc.tensor.transpose(gain_turned[:], gain_rows[:], identity_bf16[:])
+        gain = keep.tile([P, COLUMN_TILES], F32)
+        nc.vector.tensor_copy(out=gain[:], in_=gain_turned[:, 0:COLUMN_TILES])
         quantise_chunk(CHUNKS - 1, grouped_before)
 
         sums = [psum.tile([P, PIXELS], F32, tag="bank", name="sums%d" % j) for j in range(COLUMN_TILES)]

@@ -37,7 +37,8 @@ LAST_GROUPS = 4
 STREAM_GROUPS = GROUPS - LAST_GROUPS
 W_LOADS = STREAM_GROUPS // W_LOAD_GROUPS
 
-X_BUFS = 6
+HEADS_PER_TILE = P // HEAD_DIM
+X_BUFS = CHUNKS // 2
 W_BUFS = 8
 
 FLOPS = 2 * PIXELS * CHANNELS * COLUMNS
@@ -54,7 +55,7 @@ def tile_levitattention_pa_k_kernel(tc, inputs, w_qkv_words, w_qkv_scales, bn_sc
         ctx.enter_context(tc.manual_schedule())
         keep = ctx.enter_context(tc.tile_pool(name="keep", bufs=1))
         x_pool = ctx.enter_context(tc.tile_pool(name="x_pool", bufs=X_BUFS))
-        grouped_pool = ctx.enter_context(tc.tile_pool(name="grouped_pool", bufs=3))
+        grouped_pool = ctx.enter_context(tc.tile_pool(name="grouped_pool", bufs=2))
         w_pool = ctx.enter_context(tc.tile_pool(name="w_pool", bufs=W_BUFS))
         last_pool = ctx.enter_context(tc.tile_pool(name="last_pool", bufs=QUARTERS))
         psum = ctx.enter_context(tc.psum_pool(name="psum", bufs=8))
@@ -69,11 +70,16 @@ def tile_levitattention_pa_k_kernel(tc, inputs, w_qkv_words, w_qkv_scales, bn_sc
         nc.vector.memset(eps[:], BN_EPS)
         nc.vector.memset(w_planes[:].bitcast(I32), 0)
 
-        def load_chunk(c):
-            first = c * CHUNK_GROUPS * GROUP
-            x_raw = [x_pool.tile([P, CHUNK_GROUPS * GROUP], BF16, name="x_raw%d" % b) for b in range(MAPS)]
-            for b in range(MAPS):
-                nc.sync.dma_start(out=x_raw[b][:], in_=x_rows[:, b, first : first + CHUNK_GROUPS * GROUP])
+        def load_chunks(c):
+            width = 2 * CHUNK_GROUPS * GROUP
+            x_raw = x_pool.tile([P, MAPS, width], BF16, name="x_raw")
+            pieces = 2 if c == 0 else 1
+            for s in range(pieces):
+                part = slice(s * width // pieces, (s + 1) * width // pieces)
+                for b in range(MAPS):
+                    nc.sync.dma_start(
+                        out=x_raw[:, b, part], in_=x_rows[:, b, c * CHUNK_GROUPS * GROUP :][:, part]
+                    )
             return x_raw
 
         def load_scale_slot(slot):
@@ -104,8 +110,8 @@ def tile_levitattention_pa_k_kernel(tc, inputs, w_qkv_words, w_qkv_scales, bn_sc
             return w_last
 
         chunks = []
-        for c in range(X_BUFS):
-            chunks.append(load_chunk(c))
+        for c in range(0, CHUNKS, 2):
+            chunks.append(load_chunks(c))
 
         identity = keep.tile([P, P], F32)
         make_identity(nc, identity[:])
@@ -115,7 +121,7 @@ def tile_levitattention_pa_k_kernel(tc, inputs, w_qkv_words, w_qkv_scales, bn_sc
             load_scale_slot(slot)
         nc.scalar.dma_start(out=gain_rows[0:COLUMN_TILES, :], in_=bn_scale.rearrange("(j p) -> j p", p=P))
         table_warmer = keep.tile([P, 1], F32)
-        nc.scalar.sqrt(out=table_warmer[:], in_=eps[:])
+        nc.scalar.activation(out=table_warmer[:], in_=eps[:], func=ACT.Abs_reciprocal_sqrt)
 
         def quantise_chunk(c, grouped):
             groups = slice(c * CHUNK_GROUPS, (c + 1) * CHUNK_GROUPS)
@@ -131,12 +137,13 @@ def tile_levitattention_pa_k_kernel(tc, inputs, w_qkv_words, w_qkv_scales, bn_sc
                 quantise_chunk(c - 1, grouped_before)
             turned = [psum.tile([P, 2, PIXELS], F32, tag="bank", name="turned%d" % k) for k in range(CHUNK_GROUPS)]
             for b in range(MAPS):
-                words = chunks[c][b][:].bitcast(F32)
+                words = chunks[c // 2][:, b, :].bitcast(F32)
+                first = (c % 2) * CHUNK_GROUPS * GROUP_WORDS
                 for k in range(CHUNK_GROUPS):
                     for u in range(2):
                         nc.tensor.transpose(
                             turned[k][:, u, b * P : (b + 1) * P],
-                            words[:, k * GROUP_WORDS + u : (k + 1) * GROUP_WORDS : 2],
+                            words[:, first + k * GROUP_WORDS + u : first + (k + 1) * GROUP_WORDS : 2],
                             identity[:],
                         )
             grouped = grouped_pool.tile([P, CHUNK_GROUPS * PIXELS * 4], BF16, name="grouped", align_bytes=64)
@@ -151,8 +158,6 @@ def tile_levitattention_pa_k_kernel(tc, inputs, w_qkv_words, w_qkv_scales, bn_sc
                         out=pairs.rearrange("p (r u) -> p r u", u=2), in_=turned[k][:].rearrange("p u r -> p r u")
                     )
             grouped_before = grouped
-            if c + X_BUFS < CHUNKS:
-                chunks.append(load_chunk(c + X_BUFS))
 
         gain_turned = psum.tile([P, P], BF16, tag="bank", name="gain_turned")
         nc.tensor.transpose(gain_turned[:], gain_rows[:], identity_bf16[:])
@@ -183,65 +188,95 @@ def tile_levitattention_pa_k_kernel(tc, inputs, w_qkv_words, w_qkv_scales, bn_sc
                 w_tiles.append(load_weights(i + W_BUFS))
         w_lasts = [load_last_weights(quarter) for quarter in range(QUARTERS)]
 
-        result_q = keep.tile([P, MAPS * HEADS, HEAD_DIM], F32)
-        result_k = keep.tile([P, MAPS * HEADS, HEAD_DIM], F32)
-        result_v = keep.tile([P, MAPS * HEADS, 2 * HEAD_DIM], F32)
-        quarter_result = [result_q[:], result_k[:], result_v[:, :, 0:HEAD_DIM], result_v[:, :, HEAD_DIM : 2 * HEAD_DIM]]
-        complete_after = {0: (out_0, result_q), 1: (out_1, result_k), 3: (out_2, result_v)}
+        result_q = keep.tile([P, MAPS, HEADS, HEAD_DIM], F32)
+        result_k = keep.tile([P, MAPS, HEADS, HEAD_DIM], F32)
+        result_v = keep.tile([P, MAPS, HEADS, 2 * HEAD_DIM], F32)
+        quarter_result = [result_q[:], result_k[:], result_v[:, :, :, 0:HEAD_DIM], result_v[:, :, :, HEAD_DIM:]]
 
-        def finish_and_measure(quarter):
-            first = quarter * TILES_PER_QUARTER
+        def finish_and_measure(tiles):
             stats = last_pool.tile([P, TILES_PER_QUARTER, 6], F32, name="stats")
             mean_var = last_pool.tile([P, TILES_PER_QUARTER, 2], F32, name="mean_var")
-            for i in range(TILES_PER_QUARTER):
+            for i, j in enumerate(tiles):
+                quarter, column = divmod(j, TILES_PER_QUARTER)
                 for k in range(LAST_GROUPS):
-                    mx_pass(STREAM_GROUPS + k, first + i, w_lasts[quarter][:, k, i * P : (i + 1) * P])
-                nc.vector.bn_stats(out=stats[:, i, :], in_=sums[first + i][:])
+                    mx_pass(STREAM_GROUPS + k, j, w_lasts[quarter][:, k, column * P : (column + 1) * P])
+                nc.vector.bn_stats(out=stats[:, i, :], in_=sums[j][:])
                 nc.vector.bn_aggr(out=mean_var[:, i, :], in_=stats[:, i, :])
-            std = last_pool.tile([P, TILES_PER_QUARTER], F32, name="std")
-            nc.scalar.activation(out=std[:], in_=mean_var[:, :, 1], func=ACT.Sqrt, bias=eps[:, 0:1], scale=1.0)
-            return mean_var, std
-
-        def normalise(quarter, mean_var, std):
-            first = quarter * TILES_PER_QUARTER
-            factor = last_pool.tile([P, TILES_PER_QUARTER], F32, name="factor")
-            shift = last_pool.tile([P, TILES_PER_QUARTER], F32, name="shift")
-            nc.vector.reciprocal(out=factor[:], in_=std[:])
-            nc.vector.tensor_mul(out=factor[:], in0=factor[:], in1=gain[:, first : first + TILES_PER_QUARTER])
-            nc.vector.scalar_tensor_tensor(
-                out=shift[:], in0=mean_var[:, :, 0], scalar=-1.0, in1=factor[:], op0=ALU.mult, op1=ALU.mult
+            rstd = last_pool.tile([P, TILES_PER_QUARTER], F32, name="rstd")
+            n = len(tiles)
+            nc.scalar.activation(
+                out=rstd[:, 0:n], in_=mean_var[:, 0:n, 1], func=ACT.Abs_reciprocal_sqrt, bias=eps[:, 0:1], scale=1.0
             )
+            return mean_var, rstd
+
+        def normalise(tiles, mean_var, rstd):
+            n = len(tiles)
+            factor = last_pool.tile([P, TILES_PER_QUARTER], F32, name="factor")
+            nc.vector.tensor_mul(out=factor[:, 0:n], in0=rstd[:, 0:n], in1=gain[:, tiles[0] : tiles[0] + n])
             normed = last_pool.tile([P, TILES_PER_QUARTER, PIXELS], F32, name="normed")
+            if n == 2:
+                shift = last_pool.tile([P, 1], F32, name="shift")
+                nc.vector.scalar_tensor_tensor(
+                    out=shift[:], in0=mean_var[:, 1, 0:1], scalar=-1.0, in1=factor[:, 1:2], op0=ALU.mult, op1=ALU.mult
+                )
             nc.vector.tensor_scalar(
                 out=normed[:, 0, :],
-                in0=sums[first][:],
-                scalar1=factor[:, 0:1],
-                scalar2=shift[:, 0:1],
-                op0=ALU.mult,
-                op1=ALU.add,
+                in0=sums[tiles[0]][:],
+                scalar1=mean_var[:, 0, 0:1],
+                scalar2=factor[:, 0:1],
+                op0=ALU.subtract,
+                op1=ALU.mult,
             )
-            nc.scalar.activation(
-                out=normed[:, 1, :], in_=sums[first + 1][:], func=ACT.Identity, bias=shift[:, 1:2], scale=factor[:, 1:2]
-            )
+            if n == 2:
+                nc.scalar.activation(
+                    out=normed[:, 1, :], in_=sums[tiles[1]][:], func=ACT.Identity, bias=shift[:, 0:1], scale=factor[:, 1:2]
+                )
             return normed
 
-        def turn_back_and_store(quarter, normed):
-            back = psum.tile([P, MAPS, QUARTER], F32, tag="bank", name="back")
-            for i in range(TILES_PER_QUARTER):
-                for b in range(MAPS):
-                    nc.tensor.transpose(back[:, b, i * P : (i + 1) * P], normed[:, i, b * P : (b + 1) * P], identity[:])
-            nc.scalar.copy(out=quarter_result[quarter], in_=back[:].rearrange("n b (h d) -> n (b h) d", d=HEAD_DIM))
-            if quarter in complete_after:
-                out, result = complete_after[quarter]
-                nc.sync.dma_start(out=out.rearrange("b h n d -> n (b h) d"), in_=result[:])
+        def turn_back(tiles, normed):
+            for i, j in enumerate(tiles):
+                quarter, column = divmod(j, TILES_PER_QUARTER)
+                heads = slice(column * HEADS_PER_TILE, (column + 1) * HEADS_PER_TILE)
+                result = quarter_result[quarter][:, :, heads, :]
+                if j == COLUMN_TILES - 1:
+                    for b in range(MAPS):
+                        back = psum.tile([P, P], F32, tag="bank", name="back%d" % b)
+                        nc.tensor.transpose(back[:], normed[:, i, b * P : (b + 1) * P], identity[:])
+                        in_ = back[:].rearrange("n (h d) -> n h d", d=HEAD_DIM)
+                        if b == 0:
+                            nc.scalar.copy(out=result[:, b], in_=in_)
+                        else:
+                            nc.vector.tensor_copy(out=result[:, b], in_=in_)
+                else:
+                    back = psum.tile([P, MAPS, P], F32, tag="bank", name="back")
+                    for b in range(MAPS):
+                        nc.tensor.transpose(back[:, b, :], normed[:, i, b * P : (b + 1) * P], identity[:])
+                    nc.scalar.copy(out=result, in_=back[:].rearrange("n b (h d) -> n b h d", d=HEAD_DIM))
 
+        def store_pair(out, result):
+            nc.sync.dma_start(out=out.rearrange("b h n d -> n (b h) d"), in_=result[:].rearrange("n b h d -> n (b h) d"))
+
+        def store_v(column):
+            heads = slice(column * HEADS_PER_TILE, (column + 1) * HEADS_PER_TILE)
+            for b in range(MAPS):
+                nc.sync.dma_start(out=out_2[b, heads].rearrange("h n d -> n h d"), in_=result_v[:, b, heads, :])
+
+        units = [(0, 1), (2, 3), (4, 5), (6,), (7,)]
+        stores = [
+            lambda: store_pair(out_0, result_q),
+            lambda: store_pair(out_1, result_k),
+            lambda: None,
+            lambda: store_v(0),
+            lambda: store_v(1),
+        ]
         measures = {}
         normed_tiles = {}
-        for step in range(QUARTERS + 2):
-            if step < QUARTERS:
-                measures[step] = finish_and_measure(step)
-            if 0 <= step - 1 < QUARTERS:
-                mean_var, std = measures[step - 1]
-                normed_tiles[step - 1] = normalise(step - 1, mean_var, std)
-            if 0 <= step - 2 < QUARTERS:
-                turn_back_and_store(step - 2, normed_tiles[step - 2])
+        for step in range(len(units) + 2):
+            if step < len(units):
+                measures[step] = finish_and_measure(units[step])
+            if 0 <= step - 1 < len(units):
+                mean_var, rstd = measures[step - 1]
+                normed_tiles[step - 1] = normalise(units[step - 1], mean_var, rstd)
+            if 0 <= step - 2 < len(units):
+                turn_back(units[step - 2], normed_tiles[step - 2])
+                stores[step - 2]()

@@ -14,6 +14,7 @@ ACT = mybir.ActivationFunctionType
 
 P = 128
 MAPS = 2
+SIDES = 2
 PIXELS = MAPS * P
 CHANNELS = 16384
 COLUMNS = 1024
@@ -47,7 +48,7 @@ FLOPS = 2 * PIXELS * CHANNELS * COLUMNS
 def tile_levitattention_pa_k_kernel(tc, inputs, w_qkv_words, w_qkv_scales, bn_scale, out_0, out_1, out_2):
     nc = tc.nc
 
-    x_rows = inputs.rearrange("b h w c -> (h w) b c")
+    x_rows = inputs.rearrange("b h (w s) c -> (b h w) s c", s=SIDES)
     w_words = w_qkv_words.rearrange("g p n t -> g p (n t)").bitcast(I32)
     w_scale_rows = w_qkv_scales.bitcast(F32)
 
@@ -73,7 +74,7 @@ def tile_levitattention_pa_k_kernel(tc, inputs, w_qkv_words, w_qkv_scales, bn_sc
         def load_chunks(c):
             width = 2 * CHUNK_GROUPS * GROUP
             x_raw = x_pool.tile([P, MAPS, width], BF16, name="x_raw")
-            pieces = 2 if c == 0 else 1
+            pieces = 2 if c in (0, CHUNKS - 2) else 1
             for s in range(pieces):
                 part = slice(s * width // pieces, (s + 1) * width // pieces)
                 for b in range(MAPS):
@@ -158,11 +159,12 @@ def tile_levitattention_pa_k_kernel(tc, inputs, w_qkv_words, w_qkv_scales, bn_sc
                         out=pairs.rearrange("p (r u) -> p r u", u=2), in_=turned[k][:].rearrange("p u r -> p r u")
                     )
             grouped_before = grouped
+            if c == 0:
+                gain_turned = psum.tile([P, P], BF16, tag="bank", name="gain_turned")
+                nc.tensor.transpose(gain_turned[:], gain_rows[:], identity_bf16[:])
+                gain = keep.tile([P, COLUMN_TILES], F32)
+                nc.vector.tensor_copy(out=gain[:], in_=gain_turned[:, 0:COLUMN_TILES])
 
-        gain_turned = psum.tile([P, P], BF16, tag="bank", name="gain_turned")
-        nc.tensor.transpose(gain_turned[:], gain_rows[:], identity_bf16[:])
-        gain = keep.tile([P, COLUMN_TILES], F32)
-        nc.vector.tensor_copy(out=gain[:], in_=gain_turned[:, 0:COLUMN_TILES])
         quantise_chunk(CHUNKS - 1, grouped_before)
 
         sums = [psum.tile([P, PIXELS], F32, tag="bank", name="sums%d" % j) for j in range(COLUMN_TILES)]
@@ -181,16 +183,18 @@ def tile_levitattention_pa_k_kernel(tc, inputs, w_qkv_words, w_qkv_scales, bn_sc
 
         w_tiles = [load_weights(i) for i in range(W_BUFS)]
         for i in range(W_LOADS):
-            for k in range(W_LOAD_GROUPS):
-                for j in range(COLUMN_TILES):
-                    mx_pass(i * W_LOAD_GROUPS + k, j, w_tiles[i][:, k, j * P : (j + 1) * P])
+            halves = 2 if i == 0 else 1
+            for half in range(halves):
+                for k in range(W_LOAD_GROUPS):
+                    for j in range(half * COLUMN_TILES // halves, (half + 1) * COLUMN_TILES // halves):
+                        mx_pass(i * W_LOAD_GROUPS + k, j, w_tiles[i][:, k, j * P : (j + 1) * P])
             if i + W_BUFS < W_LOADS:
                 w_tiles.append(load_weights(i + W_BUFS))
         w_lasts = [load_last_weights(quarter) for quarter in range(QUARTERS)]
 
-        result_q = keep.tile([P, MAPS, HEADS, HEAD_DIM], F32)
-        result_k = keep.tile([P, MAPS, HEADS, HEAD_DIM], F32)
-        result_v = keep.tile([P, MAPS, HEADS, 2 * HEAD_DIM], F32)
+        result_q = keep.tile([P, HEADS, SIDES, HEAD_DIM], F32)
+        result_k = keep.tile([P, HEADS, SIDES, HEAD_DIM], F32)
+        result_v = keep.tile([P, HEADS, SIDES, 2 * HEAD_DIM], F32)
         quarter_result = [result_q[:], result_k[:], result_v[:, :, :, 0:HEAD_DIM], result_v[:, :, :, HEAD_DIM:]]
 
         def finish_and_measure(tiles):
@@ -237,37 +241,37 @@ def tile_levitattention_pa_k_kernel(tc, inputs, w_qkv_words, w_qkv_scales, bn_sc
             for i, j in enumerate(tiles):
                 quarter, column = divmod(j, TILES_PER_QUARTER)
                 heads = slice(column * HEADS_PER_TILE, (column + 1) * HEADS_PER_TILE)
-                result = quarter_result[quarter][:, :, heads, :]
+                result = quarter_result[quarter][:, heads, :, :]
                 if j == COLUMN_TILES - 1:
-                    for b in range(MAPS):
-                        back = psum.tile([P, P], F32, tag="bank", name="back%d" % b)
-                        nc.tensor.transpose(back[:], normed[:, i, b * P : (b + 1) * P], identity[:])
-                        in_ = back[:].rearrange("n (h d) -> n h d", d=HEAD_DIM)
-                        if b == 0:
-                            nc.scalar.copy(out=result[:, b], in_=in_)
+                    for s in range(SIDES):
+                        back = psum.tile([P, P], F32, tag="bank", name="back%d" % s)
+                        nc.tensor.transpose(back[:], normed[:, i, s * P : (s + 1) * P], identity[:])
+                        in_ = back[:].rearrange("m (h d) -> m h d", d=HEAD_DIM)
+                        if s == 0:
+                            nc.scalar.copy(out=result[:, :, s], in_=in_)
                         else:
-                            nc.vector.tensor_copy(out=result[:, b], in_=in_)
+                            nc.vector.tensor_copy(out=result[:, :, s], in_=in_)
                 else:
-                    back = psum.tile([P, MAPS, P], F32, tag="bank", name="back")
-                    for b in range(MAPS):
-                        nc.tensor.transpose(back[:, b, :], normed[:, i, b * P : (b + 1) * P], identity[:])
-                    nc.scalar.copy(out=result, in_=back[:].rearrange("n b (h d) -> n b h d", d=HEAD_DIM))
+                    back = psum.tile([P, SIDES, P], F32, tag="bank", name="back")
+                    for s in range(SIDES):
+                        nc.tensor.transpose(back[:, s, :], normed[:, i, s * P : (s + 1) * P], identity[:])
+                    nc.scalar.copy(out=result, in_=back[:].rearrange("m s (h d) -> m h s d", d=HEAD_DIM))
 
-        def store_pair(out, result):
-            nc.sync.dma_start(out=out.rearrange("b h n d -> n (b h) d"), in_=result[:].rearrange("n b h d -> n (b h) d"))
-
-        def store_v(column):
-            heads = slice(column * HEADS_PER_TILE, (column + 1) * HEADS_PER_TILE)
+        def store(out, result, heads):
             for b in range(MAPS):
-                nc.sync.dma_start(out=out_2[b, heads].rearrange("h n d -> n h d"), in_=result_v[:, b, heads, :])
+                pairs = slice(b * P // MAPS, (b + 1) * P // MAPS)
+                nc.sync.dma_start(
+                    out=out[b, heads].rearrange("h (m s) d -> m h (s d)", s=SIDES),
+                    in_=result[pairs, heads, :, :].rearrange("m h s d -> m h (s d)"),
+                )
 
         units = [(0, 1), (2, 3), (4, 5), (6,), (7,)]
         stores = [
-            lambda: store_pair(out_0, result_q),
-            lambda: store_pair(out_1, result_k),
+            lambda: store(out_0, result_q, slice(0, HEADS)),
+            lambda: store(out_1, result_k, slice(0, HEADS)),
             lambda: None,
-            lambda: store_v(0),
-            lambda: store_v(1),
+            lambda: store(out_2, result_v, slice(0, HEADS_PER_TILE)),
+            lambda: store(out_2, result_v, slice(HEADS_PER_TILE, HEADS)),
         ]
         measures = {}
         normed_tiles = {}

@@ -33,14 +33,15 @@ QUARTER = COLUMNS // QUARTERS
 TILES_PER_QUARTER = QUARTER // P
 PLANES_PER_TILE = 4
 
-W_LOAD_GROUPS = 2
+W_LOAD_GROUPS = 1
 LAST_GROUPS = 4
 STREAM_GROUPS = GROUPS - LAST_GROUPS
 W_LOADS = STREAM_GROUPS // W_LOAD_GROUPS
 
 HEADS_PER_TILE = P // HEAD_DIM
 X_BUFS = CHUNKS // 2
-W_BUFS = 8
+W_BUFS = 16
+HEAD_LOADS = 2
 
 FLOPS = 2 * PIXELS * CHANNELS * COLUMNS
 
@@ -74,7 +75,7 @@ def tile_levitattention_pa_k_kernel(tc, inputs, w_qkv_words, w_qkv_scales, bn_sc
         def load_chunks(c):
             width = 2 * CHUNK_GROUPS * GROUP
             x_raw = x_pool.tile([P, MAPS, width], BF16, name="x_raw")
-            pieces = 2 if c in (0, CHUNKS - 2) else 1
+            pieces = 2
             for s in range(pieces):
                 part = slice(s * width // pieces, (s + 1) * width // pieces)
                 for b in range(MAPS):
@@ -182,12 +183,14 @@ def tile_levitattention_pa_k_kernel(tc, inputs, w_qkv_words, w_qkv_scales, bn_sc
             )
 
         w_tiles = [load_weights(i) for i in range(W_BUFS)]
+        for half in range(2):
+            for i in range(HEAD_LOADS):
+                for j in range(half * COLUMN_TILES // 2, (half + 1) * COLUMN_TILES // 2):
+                    mx_pass(i, j, w_tiles[i][:, 0, j * P : (j + 1) * P])
         for i in range(W_LOADS):
-            halves = 2 if i == 0 else 1
-            for half in range(halves):
-                for k in range(W_LOAD_GROUPS):
-                    for j in range(half * COLUMN_TILES // halves, (half + 1) * COLUMN_TILES // halves):
-                        mx_pass(i * W_LOAD_GROUPS + k, j, w_tiles[i][:, k, j * P : (j + 1) * P])
+            if i >= HEAD_LOADS:
+                for j in range(COLUMN_TILES):
+                    mx_pass(i, j, w_tiles[i][:, 0, j * P : (j + 1) * P])
             if i + W_BUFS < W_LOADS:
                 w_tiles.append(load_weights(i + W_BUFS))
         w_lasts = [load_last_weights(quarter) for quarter in range(QUARTERS)]

@@ -62,9 +62,9 @@ def tile_levitattention_pa_k_kernel(tc, inputs, w_qkv_words, w_qkv_scales, bn_sc
         last_pool = ctx.enter_context(tc.tile_pool(name="last_pool", bufs=QUARTERS))
         psum = ctx.enter_context(tc.psum_pool(name="psum", bufs=8))
 
-        x_codes = keep.tile([P, GROUPS, PIXELS], U32, align_bytes=64)
-        x_scales = keep.tile([P, GROUPS, PIXELS], U8, align_bytes=64)
-        w_planes = keep.tile([P, GROUPS // PLANES_PER_TILE, COLUMNS], U8, align_bytes=64)
+        x_codes = keep.tile([P, GROUPS, PIXELS], U32, align_bytes=256)
+        x_scales = keep.tile([P, GROUPS, PIXELS], U8, align_bytes=256)
+        w_planes = keep.tile([P, GROUPS // PLANES_PER_TILE, COLUMNS], U8, align_bytes=256)
 
         gain_rows = keep.tile([P, P], BF16)
         nc.vector.memset(gain_rows[:], 0.0)
@@ -74,7 +74,7 @@ def tile_levitattention_pa_k_kernel(tc, inputs, w_qkv_words, w_qkv_scales, bn_sc
 
         def load_chunks(c):
             width = 2 * CHUNK_GROUPS * GROUP
-            x_raw = x_pool.tile([P, MAPS, width], BF16, name="x_raw")
+            x_raw = x_pool.tile([P, MAPS, width], BF16, name="x_raw", align_bytes=256)
             pieces = 2
             for s in range(pieces):
                 part = slice(s * width // pieces, (s + 1) * width // pieces)
@@ -93,7 +93,7 @@ def tile_levitattention_pa_k_kernel(tc, inputs, w_qkv_words, w_qkv_scales, bn_sc
                 )
 
         def load_weights(i):
-            w_tile = w_pool.tile([P, W_LOAD_GROUPS, COLUMNS], U32, name="w_tile", align_bytes=64)
+            w_tile = w_pool.tile([P, W_LOAD_GROUPS, COLUMNS], U32, name="w_tile", align_bytes=256)
             first = i * W_LOAD_GROUPS
             nc.sync.dma_start(
                 out=w_tile[:].bitcast(I32),
@@ -102,13 +102,16 @@ def tile_levitattention_pa_k_kernel(tc, inputs, w_qkv_words, w_qkv_scales, bn_sc
             return w_tile
 
         def load_last_weights(quarter):
-            w_last = last_pool.tile([P, LAST_GROUPS, QUARTER], U32, name="w_last", align_bytes=64)
-            nc.sync.dma_start(
-                out=w_last[:].bitcast(I32),
-                in_=w_words[STREAM_GROUPS:GROUPS, :, quarter * QUARTER : (quarter + 1) * QUARTER].rearrange(
-                    "g p n -> p g n"
-                ),
-            )
+            w_last = last_pool.tile([P, LAST_GROUPS, QUARTER], U32, name="w_last", align_bytes=256)
+            pieces = 2 if quarter == QUARTERS - 1 else 1
+            for k in range(0, LAST_GROUPS, LAST_GROUPS // pieces):
+                ks = slice(k, k + LAST_GROUPS // pieces)
+                nc.sync.dma_start(
+                    out=w_last[:, ks, :].bitcast(I32),
+                    in_=w_words[STREAM_GROUPS:GROUPS, :, quarter * QUARTER : (quarter + 1) * QUARTER][ks].rearrange(
+                        "g p n -> p g n"
+                    ),
+                )
             return w_last
 
         chunks = []
@@ -148,7 +151,7 @@ def tile_levitattention_pa_k_kernel(tc, inputs, w_qkv_words, w_qkv_scales, bn_sc
                             words[:, first + k * GROUP_WORDS + u : first + (k + 1) * GROUP_WORDS : 2],
                             identity[:],
                         )
-            grouped = grouped_pool.tile([P, CHUNK_GROUPS * PIXELS * 4], BF16, name="grouped", align_bytes=64)
+            grouped = grouped_pool.tile([P, CHUNK_GROUPS * PIXELS * 4], BF16, name="grouped", align_bytes=256)
             for k in range(CHUNK_GROUPS):
                 pairs = grouped[:].bitcast(F32)[:, k * 2 * PIXELS : (k + 1) * 2 * PIXELS]
                 if k < CHUNK_GROUPS - 1:
@@ -195,18 +198,25 @@ def tile_levitattention_pa_k_kernel(tc, inputs, w_qkv_words, w_qkv_scales, bn_sc
                 w_tiles.append(load_weights(i + W_BUFS))
         w_lasts = [load_last_weights(quarter) for quarter in range(QUARTERS)]
 
-        result_q = keep.tile([P, HEADS, SIDES, HEAD_DIM], F32)
-        result_k = keep.tile([P, HEADS, SIDES, HEAD_DIM], F32)
-        result_v = keep.tile([P, HEADS, SIDES, 2 * HEAD_DIM], F32)
+        result_q = keep.tile([P, HEADS, SIDES, HEAD_DIM], F32, align_bytes=256)
+        result_k = keep.tile([P, HEADS, SIDES, HEAD_DIM], F32, align_bytes=256)
+        result_v = keep.tile([P, HEADS, SIDES, 2 * HEAD_DIM], F32, align_bytes=256)
         quarter_result = [result_q[:], result_k[:], result_v[:, :, :, 0:HEAD_DIM], result_v[:, :, :, HEAD_DIM:]]
 
+        def last_passes(j, ks):
+            quarter, column = divmod(j, TILES_PER_QUARTER)
+            for k in ks:
+                mx_pass(STREAM_GROUPS + k, j, w_lasts[quarter][:, k, column * P : (column + 1) * P])
+
         def finish_and_measure(tiles):
+            first_k = 0 if len(tiles) == TILES_PER_QUARTER else LAST_GROUPS // 2
+            if tiles == (COLUMN_TILES - 2,):
+                for j in (COLUMN_TILES - 2, COLUMN_TILES - 1):
+                    last_passes(j, range(first_k))
             stats = last_pool.tile([P, TILES_PER_QUARTER, 6], F32, name="stats")
             mean_var = last_pool.tile([P, TILES_PER_QUARTER, 2], F32, name="mean_var")
             for i, j in enumerate(tiles):
-                quarter, column = divmod(j, TILES_PER_QUARTER)
-                for k in range(LAST_GROUPS):
-                    mx_pass(STREAM_GROUPS + k, j, w_lasts[quarter][:, k, column * P : (column + 1) * P])
+                last_passes(j, range(first_k, LAST_GROUPS))
                 nc.vector.bn_stats(out=stats[:, i, :], in_=sums[j][:])
                 nc.vector.bn_aggr(out=mean_var[:, i, :], in_=stats[:, i, :])
             rstd = last_pool.tile([P, TILES_PER_QUARTER], F32, name="rstd")

@@ -41,6 +41,7 @@ W_LOADS = STREAM_GROUPS // W_LOAD_GROUPS
 HEADS_PER_TILE = P // HEAD_DIM
 X_BUFS = CHUNKS // 2
 W_BUFS = 16
+EARLY_SLOTS = 2
 HEAD_LOADS = 2
 
 FLOPS = 2 * PIXELS * CHANNELS * COLUMNS
@@ -75,13 +76,15 @@ def tile_levitattention_pa_k_kernel(tc, inputs, w_qkv_words, w_qkv_scales, bn_sc
         def load_chunks(c):
             width = 2 * CHUNK_GROUPS * GROUP
             x_raw = x_pool.tile([P, MAPS, width], BF16, name="x_raw", align_bytes=256)
-            pieces = 2
-            for s in range(pieces):
-                part = slice(s * width // pieces, (s + 1) * width // pieces)
+            half = width // 2
+            for i in range(2):
                 for b in range(MAPS):
-                    nc.sync.dma_start(
-                        out=x_raw[:, b, part], in_=x_rows[:, b, c * CHUNK_GROUPS * GROUP :][:, part]
-                    )
+                    pieces = 2 if (c, i, b) == (CHUNKS - 2, 1, MAPS - 1) else 1
+                    for k in range(pieces):
+                        part = slice(i * half + k * half // pieces, i * half + (k + 1) * half // pieces)
+                        nc.sync.dma_start(
+                            out=x_raw[:, b, part], in_=x_rows[:, b, c * CHUNK_GROUPS * GROUP :][:, part]
+                        )
             return x_raw
 
         def load_scale_slot(slot):
@@ -122,7 +125,11 @@ def tile_levitattention_pa_k_kernel(tc, inputs, w_qkv_words, w_qkv_scales, bn_sc
         make_identity(nc, identity[:])
         identity_bf16 = keep.tile([P, P], BF16)
         make_identity(nc, identity_bf16[:])
-        for slot in range(GROUPS // PLANES_PER_TILE):
+        for slot in range(EARLY_SLOTS):
+            load_scale_slot(slot)
+        pace = keep.tile([P, 1], BF16)
+        nc.gpsimd.tensor_copy(out=pace[:], in_=chunks[-1][:, 0, 2 * CHUNK_GROUPS * GROUP - 1 :])
+        for slot in range(EARLY_SLOTS, GROUPS // PLANES_PER_TILE):
             load_scale_slot(slot)
         nc.scalar.dma_start(out=gain_rows[0:COLUMN_TILES, :], in_=bn_scale.rearrange("(j p) -> j p", p=P))
         table_warmer = keep.tile([P, 1], F32)
@@ -215,8 +222,12 @@ def tile_levitattention_pa_k_kernel(tc, inputs, w_qkv_words, w_qkv_scales, bn_sc
                     last_passes(j, range(first_k))
             stats = last_pool.tile([P, TILES_PER_QUARTER, 6], F32, name="stats")
             mean_var = last_pool.tile([P, TILES_PER_QUARTER, 2], F32, name="mean_var")
+            if tiles == (COLUMN_TILES - 2,):
+                for j in (COLUMN_TILES - 2, COLUMN_TILES - 1):
+                    last_passes(j, range(first_k, LAST_GROUPS))
             for i, j in enumerate(tiles):
-                last_passes(j, range(first_k, LAST_GROUPS))
+                if len(tiles) == TILES_PER_QUARTER:
+                    last_passes(j, range(first_k, LAST_GROUPS))
                 nc.vector.bn_stats(out=stats[:, i, :], in_=sums[j][:])
                 nc.vector.bn_aggr(out=mean_var[:, i, :], in_=stats[:, i, :])
             rstd = last_pool.tile([P, TILES_PER_QUARTER], F32, name="rstd")

from contextlib import ExitStack

import concourse.mybir as mybir
from concourse.masks import make_identity

F32 = mybir.dt.float32
BF16 = mybir.dt.bfloat16
I32 = mybir.dt.int32
U32 = mybir.dt.uint32
U8 = mybir.dt.uint8
FP8X4 = mybir.dt.float8_e4m3fn_x4
ALU = mybir.AluOpType
ACT = mybir.ActivationFunctionType

P = 128
MAPS = 2
SIDES = 2
PIXELS = MAPS * P
CHANNELS = 16384
COLUMNS = 1024
HEADS = 8
HEAD_DIM = 32
BN_EPS = 1e-5

GROUP = 4 * P
GROUPS = CHANNELS // GROUP
GROUP_WORDS = GROUP // 2
CHUNK_GROUPS = 4
CHUNKS = GROUPS // CHUNK_GROUPS
COLUMN_TILES = COLUMNS // P
QUARTERS = 4
QUARTER = COLUMNS // QUARTERS
TILES_PER_QUARTER = QUARTER // P
PLANES_PER_TILE = 4

W_LOAD_GROUPS = 1
LAST_GROUPS = 4
STREAM_GROUPS = GROUPS - LAST_GROUPS
W_LOADS = STREAM_GROUPS // W_LOAD_GROUPS

HEADS_PER_TILE = P // HEAD_DIM
X_BUFS = CHUNKS // 2
W_BUFS = 16
EARLY_SLOTS = 2
HEAD_LOADS = 2

FLOPS = 2 * PIXELS * CHANNELS * COLUMNS


def tile_levitattention_pa_k_kernel(tc, inputs, w_qkv_words, w_qkv_scales, bn_scale, out_0, out_1, out_2):
    nc = tc.nc

    x_rows = inputs.rearrange("b h (w s) c -> (b h w) s c", s=SIDES)
    w_words = w_qkv_words.rearrange("g p n t -> g p (n t)").bitcast(I32)
    w_scale_rows = w_qkv_scales.bitcast(F32)

    with ExitStack() as ctx:
        ctx.enter_context(tc.manual_schedule())
        keep = ctx.enter_context(tc.tile_pool(name="keep", bufs=1))
        x_pool = ctx.enter_context(tc.tile_pool(name="x_pool", bufs=X_BUFS))
        grouped_pool = ctx.enter_context(tc.tile_pool(name="grouped_pool", bufs=2))
        w_pool = ctx.enter_context(tc.tile_pool(name="w_pool", bufs=W_BUFS))
        last_pool = ctx.enter_context(tc.tile_pool(name="last_pool", bufs=QUARTERS))
        psum = ctx.enter_context(tc.psum_pool(name="psum", bufs=8))

        x_codes = keep.tile([P, GROUPS, PIXELS], U32, align_bytes=256)
        x_scales = keep.tile([P, GROUPS, PIXELS], U8, align_bytes=256)
        w_planes = keep.tile([P, GROUPS // PLANES_PER_TILE, COLUMNS], U8, align_bytes=256)

        gain_rows = keep.tile([P, P], BF16)
        nc.vector.memset(gain_rows[:], 0.0)
        eps = keep.tile([P, 1], F32)
        nc.vector.memset(eps[:], BN_EPS)
        nc.vector.memset(w_planes[:].bitcast(I32), 0)

        def load_chunks(c):
            width = 2 * CHUNK_GROUPS * GROUP
            x_raw = x_pool.tile([P, MAPS, width], BF16, name="x_raw", align_bytes=256)
            half = width // 2
            for i in range(2):
                for b in range(MAPS):
                    pieces = 2 if (c, i, b) == (CHUNKS - 2, 1, MAPS - 1) else 1
                    for k in range(pieces):
                        part = slice(i * half + k * half // pieces, i * half + (k + 1) * half // pieces)
                        nc.sync.dma_start(
                            out=x_raw[:, b, part], in_=x_rows[:, b, c * CHUNK_GROUPS * GROUP :][:, part]
                        )
            return x_raw

        def load_scale_slot(slot):
            first = slot * PLANES_PER_TILE
            for quadrant in range(4):
                nc.gpsimd.dma_start(
                    out=w_planes[32 * quadrant : 32 * quadrant + 16, slot, :].bitcast(F32),
                    in_=w_scale_rows[first : first + PLANES_PER_TILE, 4 * quadrant : 4 * quadrant + 4, :],
                )

        def load_weights(i):
            w_tile = w_pool.tile([P, W_LOAD_GROUPS, COLUMNS], U32, name="w_tile", align_bytes=256)
            first = i * W_LOAD_GROUPS
            nc.sync.dma_start(
                out=w_tile[:].bitcast(I32),
                in_=w_words[first : first + W_LOAD_GROUPS].rearrange("g p n -> p g n"),
            )
            return w_tile

        def load_last_weights(quarter):
            w_last = last_pool.tile([P, LAST_GROUPS, QUARTER], U32, name="w_last", align_bytes=256)
            pieces = 2 if quarter == QUARTERS - 1 else 1
            for k in range(0, LAST_GROUPS, LAST_GROUPS // pieces):
                ks = slice(k, k + LAST_GROUPS // pieces)
                nc.sync.dma_start(
                    out=w_last[:, ks, :].bitcast(I32),
                    in_=w_words[STREAM_GROUPS:GROUPS, :, quarter * QUARTER : (quarter + 1) * QUARTER][ks].rearrange(
                        "g p n -> p g n"
                    ),
                )
            return w_last

        chunks = []
        for c in range(0, CHUNKS, 2):
            chunks.append(load_chunks(c))

        identity = keep.tile([P, P], F32)
        make_identity(nc, identity[:])
        identity_bf16 = keep.tile([P, P], BF16)
        make_identity(nc, identity_bf16[:])
        for slot in range(EARLY_SLOTS):
            load_scale_slot(slot)
        pace = keep.tile([P, 1], BF16)
        nc.gpsimd.tensor_copy(out=pace[:], in_=chunks[-1][:, 0, 2 * CHUNK_GROUPS * GROUP - 1 :])
        for slot in range(EARLY_SLOTS, GROUPS // PLANES_PER_TILE):
            load_scale_slot(slot)
        nc.scalar.dma_start(out=gain_rows[0:COLUMN_TILES, :], in_=bn_scale.rearrange("(j p) -> j p", p=P))
        table_warmer = keep.tile([P, 1], F32)
        nc.scalar.activation(out=table_warmer[:], in_=eps[:], func=ACT.Abs_reciprocal_sqrt)

        def quantise_chunk(c, grouped):
            groups = slice(c * CHUNK_GROUPS, (c + 1) * CHUNK_GROUPS)
            nc.vector.quantize_mx(
                out=x_codes[:, groups, :].rearrange("p g r -> p (g r)").bitcast(FP8X4),
                scales=x_scales[:, groups, :].rearrange("p g r -> p (g r)"),
                in_=grouped[:],
            )

        grouped_before = None
        for c in range(CHUNKS):
            if grouped_before is not None:
                quantise_chunk(c - 1, grouped_before)
            turned = [psum.tile([P, 2, PIXELS], F32, tag="bank", name="turned%d" % k) for k in range(CHUNK_GROUPS)]
            for b in range(MAPS):
                words = chunks[c // 2][:, b, :].bitcast(F32)
                first = (c % 2) * CHUNK_GROUPS * GROUP_WORDS
                for k in range(CHUNK_GROUPS):
                    for u in range(2):
                        nc.tensor.transpose(
                            turned[k][:, u, b * P : (b + 1) * P],
                            words[:, first + k * GROUP_WORDS + u : first + (k + 1) * GROUP_WORDS : 2],
                            identity[:],
                        )
            grouped = grouped_pool.tile([P, CHUNK_GROUPS * PIXELS * 4], BF16, name="grouped", align_bytes=256)
            for k in range(CHUNK_GROUPS):
                pairs = grouped[:].bitcast(F32)[:, k * 2 * PIXELS : (k + 1) * 2 * PIXELS]
                if k < CHUNK_GROUPS - 1:
                    nc.scalar.copy(
                        out=pairs.rearrange("p (r u) -> p r u", u=2), in_=turned[k][:].rearrange("p u r -> p r u")
                    )
                else:
                    nc.vector.tensor_copy(
                        out=pairs.rearrange("p (r u) -> p r u", u=2), in_=turned[k][:].rearrange("p u r -> p r u")
                    )
            grouped_before = grouped
            if c == 0:
                gain_turned = psum.tile([P, P], BF16, tag="bank", name="gain_turned")
                nc.tensor.transpose(gain_turned[:], gain_rows[:], identity_bf16[:])
                gain = keep.tile([P, COLUMN_TILES], F32)
                nc.vector.tensor_copy(out=gain[:], in_=gain_turned[:, 0:COLUMN_TILES])

        quantise_chunk(CHUNKS - 1, grouped_before)

        sums = [psum.tile([P, PIXELS], F32, tag="bank", name="sums%d" % j) for j in range(COLUMN_TILES)]

        def mx_pass(g, j, w_columns):
            plane = PLANES_PER_TILE * (g % PLANES_PER_TILE)
            nc.tensor.matmul_mx(
                out=sums[j][:],
                lhsT=w_columns.bitcast(FP8X4),
                lhsT_scale=w_planes[plane:P, g // PLANES_PER_TILE, j * P : (j + 1) * P],
                rhs=x_codes[:, g, :].bitcast(FP8X4),
                rhs_scale=x_scales[:, g, :],
                start=(g == 0),
                stop=(g == GROUPS - 1),
            )

        w_tiles = [load_weights(i) for i in range(W_BUFS)]
        for half in range(2):
            for i in range(HEAD_LOADS):
                for j in range(half * COLUMN_TILES // 2, (half + 1) * COLUMN_TILES // 2):
                    mx_pass(i, j, w_tiles[i][:, 0, j * P : (j + 1) * P])
        for i in range(W_LOADS):
            if i >= HEAD_LOADS:
                for j in range(COLUMN_TILES):
                    mx_pass(i, j, w_tiles[i][:, 0, j * P : (j + 1) * P])
            if i + W_BUFS < W_LOADS:
                w_tiles.append(load_weights(i + W_BUFS))
        w_lasts = [load_last_weights(quarter) for quarter in range(QUARTERS)]

        result_q = keep.tile([P, HEADS, SIDES, HEAD_DIM], F32, align_bytes=256)
        result_k = keep.tile([P, HEADS, SIDES, HEAD_DIM], F32, align_bytes=256)
        result_v = keep.tile([P, HEADS, SIDES, 2 * HEAD_DIM], F32, align_bytes=256)
        quarter_result = [result_q[:], result_k[:], result_v[:, :, :, 0:HEAD_DIM], result_v[:, :, :, HEAD_DIM:]]

        def last_passes(j, ks):
            quarter, column = divmod(j, TILES_PER_QUARTER)
            for k in ks:
                mx_pass(STREAM_GROUPS + k, j, w_lasts[quarter][:, k, column * P : (column + 1) * P])

        def finish_and_measure(tiles):
            first_k = 0 if len(tiles) == TILES_PER_QUARTER else LAST_GROUPS // 2
            if tiles == (COLUMN_TILES - 2,):
                for j in (COLUMN_TILES - 2, COLUMN_TILES - 1):
                    last_passes(j, range(first_k))
            stats = last_pool.tile([P, TILES_PER_QUARTER, 6], F32, name="stats")
            mean_var = last_pool.tile([P, TILES_PER_QUARTER, 2], F32, name="mean_var")
            if tiles == (COLUMN_TILES - 2,):
                for j in (COLUMN_TILES - 2, COLUMN_TILES - 1):
                    last_passes(j, range(first_k, LAST_GROUPS))
            for i, j in enumerate(tiles):
                if len(tiles) == TILES_PER_QUARTER:
                    last_passes(j, range(first_k, LAST_GROUPS))
                nc.vector.bn_stats(out=stats[:, i, :], in_=sums[j][:])
                nc.vector.bn_aggr(out=mean_var[:, i, :], in_=stats[:, i, :])
            rstd = last_pool.tile([P, TILES_PER_QUARTER], F32, name="rstd")
            n = len(tiles)
            nc.scalar.activation(
                out=rstd[:, 0:n], in_=mean_var[:, 0:n, 1], func=ACT.Abs_reciprocal_sqrt, bias=eps[:, 0:1], scale=1.0
            )
            return mean_var, rstd

        def normalise(tiles, mean_var, rstd):
            n = len(tiles)
            factor = last_pool.tile([P, TILES_PER_QUARTER], F32, name="factor")
            nc.vector.tensor_mul(out=factor[:, 0:n], in0=rstd[:, 0:n], in1=gain[:, tiles[0] : tiles[0] + n])
            normed = last_pool.tile([P, TILES_PER_QUARTER, PIXELS], F32, name="normed")
            if n == 2:
                shift = last_pool.tile([P, 1], F32, name="shift")
                nc.vector.scalar_tensor_tensor(
                    out=shift[:], in0=mean_var[:, 1, 0:1], scalar=-1.0, in1=factor[:, 1:2], op0=ALU.mult, op1=ALU.mult
                )
            nc.vector.tensor_scalar(
                out=normed[:, 0, :],
                in0=sums[tiles[0]][:],
                scalar1=mean_var[:, 0, 0:1],
                scalar2=factor[:, 0:1],
                op0=ALU.subtract,
                op1=ALU.mult,
            )
            if n == 2:
                nc.scalar.activation(
                    out=normed[:, 1, :], in_=sums[tiles[1]][:], func=ACT.Identity, bias=shift[:, 0:1], scale=factor[:, 1:2]
                )
            return normed

        def turn_back(tiles, normed):
            for i, j in enumerate(tiles):
                quarter, column = divmod(j, TILES_PER_QUARTER)
                heads = slice(column * HEADS_PER_TILE, (column + 1) * HEADS_PER_TILE)
                result = quarter_result[quarter][:, heads, :, :]
                if j == COLUMN_TILES - 1:
                    for s in range(SIDES):
                        back = psum.tile([P, P], F32, tag="bank", name="back%d" % s)
                        nc.tensor.transpose(back[:], normed[:, i, s * P : (s + 1) * P], identity[:])
                        in_ = back[:].rearrange("m (h d) -> m h d", d=HEAD_DIM)
                        if s == 0:
                            nc.scalar.copy(out=result[:, :, s], in_=in_)
                        else:
                            nc.vector.tensor_copy(out=result[:, :, s], in_=in_)
                else:
                    back = psum.tile([P, SIDES, P], F32, tag="bank", name="back")
                    for s in range(SIDES):
                        nc.tensor.transpose(back[:, s, :], normed[:, i, s * P : (s + 1) * P], identity[:])
                    nc.scalar.copy(out=result, in_=back[:].rearrange("m s (h d) -> m h s d", d=HEAD_DIM))

        def store(out, result, heads):
            for b in range(MAPS):
                pairs = slice(b * P // MAPS, (b + 1) * P // MAPS)
                nc.sync.dma_start(
                    out=out[b, heads].rearrange("h (m s) d -> m h (s d)", s=SIDES),
                    in_=result[pairs, heads, :, :].rearrange("m h s d -> m h (s d)"),
                )

        units = [(0, 1), (2, 3), (4, 5), (6,), (7,)]
        stores = [
            lambda: store(out_0, result_q, slice(0, HEADS)),
            lambda: store(out_1, result_k, slice(0, HEADS)),
            lambda: None,
            lambda: store(out_2, result_v, slice(0, HEADS_PER_TILE)),
            lambda: store(out_2, result_v, slice(HEADS_PER_TILE, HEADS)),
        ]
        measures = {}
        normed_tiles = {}
        for step in range(len(units) + 2):
            if step < len(units):
                measures[step] = finish_and_measure(units[step])
            if 0 <= step - 1 < len(units):
                mean_var, rstd = measures[step - 1]
                normed_tiles[step - 1] = normalise(units[step - 1], mean_var, rstd)
            if 0 <= step - 2 < len(units):
                turn_back(units[step - 2], normed_tiles[step - 2])
                stores[step - 2]()
